import numpy as np
import ml_dtypes


def mxq(x, axis, fmt="e4m3"):
    dtype, down = {"e4m3": (ml_dtypes.float8_e4m3fn, 7), "e5m2": (ml_dtypes.float8_e5m2, 14)}[fmt]
    v = np.moveaxis(np.asarray(x, np.float32).astype(ml_dtypes.bfloat16).astype(np.float64), axis, -1)
    blocks = v.reshape(v.shape[:-1] + (-1, 32))
    amax = np.abs(blocks).max(-1, keepdims=True)
    byte = np.maximum(np.where(amax > 0, np.frexp(amax)[1] - 1 + 127, 0) - down, 1)
    scale = np.exp2(byte - 127.0)
    codes = (blocks / scale).astype(np.float32).astype(dtype).astype(np.float64)
    return np.moveaxis((codes * scale).reshape(v.shape), -1, axis)


WIDE = False


def mx_kscale(k):
    if not WIDE:
        return np.ones(k)
    levels = np.array([10, -10, 5, -5, 0])
    if k % 512:
        return np.exp2(np.random.permutation(np.resize(levels, k // 32))).repeat(32)
    a = np.empty((k // 512, 16))
    for p in range(k // 512):
        a[p, :8] = np.random.permutation(np.resize(levels, 8))
        for g in range(8):
            far = levels[np.abs(levels - a[p, g]) >= 10]
            a[p, g + 8] = far[np.random.randint(len(far))]
    return np.exp2(a.ravel()).repeat(32)


BF16 = ml_dtypes.bfloat16


def bf(x):
    return np.asarray(x, np.float32).astype(BF16)


def f64(x):
    return np.asarray(x).astype(np.float64)


B, CIN, CM, CO, H, WD = 1, 512, 512, 512, 16, 16
RING = [(-1, -1), (-1, 0), (-1, 1), (0, 1), (1, 1), (1, 0), (1, -1), (0, -1)]
NUM_K = 9
KERNEL_ROT = 4
STEP = 2
M = NUM_K * CM


def setup_inputs():
    s = mx_kscale(CIN)
    t = mx_kscale(CM)
    return {"x": bf(np.random.standard_normal((B, CIN, H, WD)) * s[None, :, None, None]),
            "W": bf(np.random.standard_normal((CM, CIN, NUM_K)) / np.sqrt(CIN) / s[None, :, None] * t[:, None, None]),
            "W1": bf(np.random.standard_normal((CO, M)) * 1.4 / np.sqrt(M) / np.tile(t, NUM_K)[None, :])}


def reference(x, W, W1):
    xq = mxq(f64(x), 1, "e4m3")
    Wq = mxq(f64(W), 1, "e4m3")
    z = f64(bf(Wq.transpose(0, 2, 1).reshape(CM * NUM_K, CIN) @ xq.reshape(B, CIN, H * WD))).reshape(B, CM, NUM_K, H, WD)
    h = np.maximum(z, 0.0)
    hq = mxq(h, 1, "e4m3")
    W1q = mxq(f64(W1).reshape(CO, NUM_K, CM), 2, "e4m3")
    u = (W1q.transpose(1, 0, 2) @ hq.transpose(0, 2, 1, 3, 4).reshape(B, NUM_K, CM, H * WD)).reshape(B, NUM_K, CO, H, WD)
    up = np.pad(u, ((0, 0), (0, 0), (0, 0), (1, 1), (1, 1)))
    rot_out = []
    for rot in range(KERNEL_ROT):
        roff = STEP * rot
        acc = 0.0
        for k in range(NUM_K):
            dy, dx = (0, 0) if k == NUM_K - 1 else RING[(k + roff) % len(RING)]
            acc = acc + up[:, k, :, 1 + dy:1 + dy + H, 1 + dx:1 + dx + WD]
        rot_out.append(acc)
    return np.stack(rot_out, axis=2)

@@ -1,0 +1,289 @@
+from contextlib import ExitStack
+
+import concourse.mybir as mybir
+from concourse.masks import make_identity
+
+F32 = mybir.dt.float32
+BF16 = mybir.dt.bfloat16
+U32 = mybir.dt.uint32
+U8 = mybir.dt.uint8
+FP8X4 = mybir.dt.float8_e4m3fn_x4
+RELU = mybir.ActivationFunctionType.Relu
+
+P = 128
+NK = 9
+HW = 256
+ROW = 64
+RING = [(-1, -1), (-1, 0), (-1, 1), (0, 1), (1, 1), (1, 0), (1, -1), (0, -1)]
+NSET = 3
+N_H0 = 5
+N_WARM = 8
+Z_DT = BF16
+C_TILES = [(0, 2), (2, 2), (4, 2), (6, 2), (8, 1)]
+
+FLOPS = 2 * 2 * NK * 512 * 512 * HW
+
+
+def tile_psr4convf_kernel(tc, x, W, W1, out):
+    nc = tc.nc
+    x_v = x[0].rearrange("(p j) h w -> p j (h w)", j=4)
+    w_v = W.rearrange("(m t) c k -> m t (c k)", t=4)
+    w1_v = W1.rearrange("(m q) f -> m q f", q=4)
+    out_v = out[0].rearrange("(m q) r h w -> m q (r h w)", q=4)
+
+    with ExitStack() as ctx:
+        const = ctx.enter_context(tc.tile_pool(name="const", bufs=1))
+        raw = ctx.enter_context(tc.tile_pool(name="raw", bufs=4))
+        regr = ctx.enter_context(tc.tile_pool(name="regr", bufs=2))
+        stage = ctx.enter_context(tc.tile_pool(name="stage", bufs=5))
+        outp = ctx.enter_context(tc.tile_pool(name="outp", bufs=4))
+        work = ctx.enter_context(tc.psum_pool(name="work", bufs=8))
+
+        wraw = []
+        for t in range(4):
+            r = raw.tile([P, NK * 512], BF16, name="wraw%d" % t, tag="raw")
+            nc.sync.dma_start(out=r[:], in_=w_v[:, t, :])
+            wraw.append(r)
+        xraw = const.tile([P, 4, HW], BF16, name="xraw")
+        nc.sync.dma_start(out=xraw[:], in_=x_v)
+        w1raw = []
+
+        def load_w1(q):
+            r1 = raw.tile([P, NK * 512], BF16, name="w1raw%d" % q, tag="raw")
+            nc.sync.dma_start(out=r1[:], in_=w1_v[:, q, :])
+            w1raw.append(r1)
+
+        dummy = const.tile([P, 512], BF16, name="dummy")
+        nc.vector.memset(dummy[:], 0.0)
+        ident_f = const.tile([P, P], F32, name="ident_f")
+        make_identity(nc, ident_f[:])
+        h0s = []
+        for k in range(N_H0):
+            h0k = const.tile([P, 18, 16, 4], BF16, name="h0_%d" % k, align_bytes=64)
+            nc.vector.memset(h0k[:, 0:18:17, :, :], 0.0)
+            h0s.append(h0k)
+        hset = []
+        for s in range(NSET):
+            pair = []
+            for nm in ("hp", "hm"):
+                ht = const.tile([P, 18, 16, 4], BF16, name="%s_%d" % (nm, s), align_bytes=64)
+                nc.vector.memset(ht[:], 0.0)
+                pair.append(ht)
+            hset.append(pair)
+        warm = const.tile([P, 1], F32, name="warm")
+        nc.vector.memset(warm[:], 0.0)
+        nc.scalar.activation(out=warm[:], in_=warm[:], func=RELU)
+
+        xg = const.tile([P, HW, 4], BF16, name="xg", align_bytes=64)
+        xc = const.tile([P, HW], U32, name="xc", align_bytes=64)
+        xs = const.tile([P, HW], U8, name="xs", align_bytes=64)
+        wc = const.tile([P, 4 * NK * P], U32, name="wc", align_bytes=64)
+        ws = const.tile([P, 4 * NK * P], U8, name="ws", align_bytes=64)
+        w1c = const.tile([P, 4 * NK * P], U32, name="w1c", align_bytes=64)
+        w1s = const.tile([P, 4 * NK * P], U8, name="w1s", align_bytes=64)
+        hc = []
+        hs = []
+        for k in range(NK):
+            nver = 4 if k < 8 else 2
+            hck = const.tile([P, nver * HW], U32, name="hc%d" % k, align_bytes=64)
+            hsk = const.tile([P, nver * HW], U8, name="hs%d" % k, align_bytes=64)
+            hc.append(hck)
+            hs.append(hsk)
+
+        def x_prep():
+            nc.vector.tensor_copy(out=xg[:], in_=xraw[:].rearrange("p j n -> p n j"))
+            nc.vector.quantize_mx(out=xc[:].bitcast(FP8X4), scales=xs[:], in_=xg[:].rearrange("p n j -> p (n j)"))
+
+        def quantize_piece(grouped, codes, scales, chunk, k0, k1):
+            c0 = (chunk * NK + k0) * P
+            c1 = (chunk * NK + k1) * P
+            nc.vector.quantize_mx(
+                out=codes[:, c0:c1].bitcast(FP8X4),
+                scales=scales[:, c0:c1],
+                in_=grouped[:, k0 * 512 : k1 * 512],
+            )
+
+        def burst(n, lhs, rhs):
+            wps = work.tile([P, 512], F32, name="wps", tag="bank")
+            for i in range(n):
+                nc.tensor.matmul(out=wps[:], lhsT=lhs, rhs=rhs, start=True, stop=True)
+
+        wgs = {}
+
+        def transposed(words, grouped):
+            for k0, nk in C_TILES:
+                tp1 = work.tile([P, 2, 2, P], F32, name="tp1", tag="bank")
+                for kk in range(nk):
+                    for u in range(2):
+                        nc.tensor.transpose(out=tp1[:, kk, u, :], in_=words[:, k0 + kk, u, :], identity=ident_f[:])
+                dst = (
+                    grouped[:, k0 * 512 : (k0 + nk) * 512]
+                    .bitcast(F32)
+                    .rearrange("p (k m u) -> p k m u", k=nk, u=2)
+                )
+                nc.scalar.copy(out=dst, in_=tp1[:, 0:nk, :, :].rearrange("p k u m -> p k m u"))
+
+        def w_tiles(t):
+            wk = regr.tile([P, NK, 2, P, 2], BF16, name="wk", tag="wk")
+            src = wraw[t][:].rearrange("m (a u e k) -> m k u a e", u=2, e=2, k=NK)
+            for k0, k1 in ((0, 4), (4, 8)):
+                for u in range(2):
+                    nc.vector.tensor_copy(out=wk[:, k0:k1, u, :, :], in_=src[:, k0:k1, u, :, :])
+            for u in range(2):
+                nc.scalar.copy(out=wk[:, 8, u, :, :], in_=src[:, 8, u, :, :])
+            wg = stage.tile([P, NK * 512], BF16, name="wg", tag="grouped", align_bytes=64)
+            wgs[t] = wg
+            words = wk[:].rearrange("m k u a e -> m (k u a e)").bitcast(F32).rearrange("m (k u a) -> m k u a", k=NK, u=2)
+            transposed(words, wg)
+
+        def w_quant(t):
+            quantize_piece(wgs[t], wc, ws, t, 0, 4)
+            quantize_piece(wgs[t], wc, ws, t, 4, 8)
+            quantize_piece(wgs[t], wc, ws, t, 8, 9)
+
+        def c_run(q):
+            w1g = stage.tile([P, NK * 512], BF16, name="w1g", tag="grouped", align_bytes=64)
+            words = w1raw[q][:].bitcast(F32).rearrange("m (k a u) -> m k u a", k=NK, u=2)
+            for k0, nk in C_TILES:
+                tp1 = work.tile([P, 2, 2, P], F32, name="tp1", tag="bank")
+                for kk in range(nk):
+                    for u in range(2):
+                        nc.tensor.transpose(out=tp1[:, kk, u, :], in_=words[:, k0 + kk, u, :], identity=ident_f[:])
+                dst = (
+                    w1g[:, k0 * 512 : (k0 + nk) * 512]
+                    .bitcast(F32)
+                    .rearrange("p (k m u) -> p k m u", k=nk, u=2)
+                )
+                nc.scalar.copy(out=dst, in_=tp1[:, 0:nk, :, :].rearrange("p k u m -> p k m u"))
+                if k0 == 2:
+                    quantize_piece(w1g, w1c, w1s, q, 0, 4)
+                if k0 == 6:
+                    quantize_piece(w1g, w1c, w1s, q, 4, 8)
+            quantize_piece(w1g, w1c, w1s, q, 8, 9)
+
+        set_of = {}
+
+        def stage1(k):
+            set_of[k] = hset[k % NSET]
+            h0 = h0s[k % N_H0]
+            hp, hm = set_of[k]
+            h0f = h0[:].rearrange("p a b t -> p (a b t)")
+            for nh in range(2):
+                z = work.tile([P, 4, P], Z_DT, name="z", tag="bank")
+                for t in range(4):
+                    c0 = (t * NK + k) * P
+                    nc.tensor.matmul_mx(
+                        out=z[:, t, :],
+                        lhsT=wc[:, c0 : c0 + P].bitcast(FP8X4),
+                        lhsT_scale=ws[:, c0 : c0 + P],
+                        rhs=xc[:, nh * P : (nh + 1) * P].bitcast(FP8X4),
+                        rhs_scale=xs[:, nh * P : (nh + 1) * P],
+                        start=True,
+                        stop=True,
+                    )
+                nc.scalar.activation(
+                    out=h0f[:, ROW + nh * 512 : ROW + (nh + 1) * 512].rearrange("p (n t) -> p n t", t=4),
+                    in_=z[:].rearrange("p t n -> p n t"),
+                    func=RELU,
+                )
+            if k < 8:
+                nc.vector.tensor_copy(out=hp[:, 1:17, 0:15, :], in_=h0[:, 1:17, 1:16, :])
+                nc.vector.tensor_copy(out=hm[:, 1:17, 1:16, :], in_=h0[:, 1:17, 0:15, :])
+
+        def versions(k, which):
+            h0 = h0s[k % N_H0]
+            hp, hm = set_of[k]
+            by_dx = {0: h0, 1: hp, -1: hm}
+            for v in which:
+                dy, dx = RING[(k + 2 * v) % 8] if k < 8 else (0, 0)
+                flat = by_dx[dx][:].rearrange("p a b t -> p (a b t)")
+                nc.vector.quantize_mx(
+                    out=hc[k][:, v * HW : (v + 1) * HW].bitcast(FP8X4),
+                    scales=hs[k][:, v * HW : (v + 1) * HW],
+                    in_=flat[:, (1 + dy) * ROW : (1 + dy) * ROW + 4 * HW],
+                )
+
+        accs = {}
+
+        def open_group(q, rp):
+            acc = work.tile([P, 512], F32, name="acc", tag="bank")
+            accs[(q, rp)] = acc
+
+        def stage2(q, rp, k, first_pass, last_pass):
+            c0 = (q * NK + k) * P
+            r0 = rp * 512 if k < 8 else 0
+            nc.tensor.matmul_mx(
+                out=accs[(q, rp)][:],
+                lhsT=w1c[:, c0 : c0 + P].bitcast(FP8X4),
+                lhsT_scale=w1s[:, c0 : c0 + P],
+                rhs=hc[k][:, r0 : r0 + 512].bitcast(FP8X4),
+                rhs_scale=hs[k][:, r0 : r0 + 512],
+                start=first_pass,
+                stop=last_pass,
+            )
+
+        def finish_group(q, rp):
+            osb = outp.tile([P, 512], F32, name="osb", tag="osb")
+            if q % 2 == 0:
+                nc.vector.tensor_copy(out=osb[:], in_=accs[(q, rp)][:])
+            else:
+                nc.scalar.copy(out=osb[:], in_=accs[(q, rp)][:])
+            nc.sync.dma_start(out=out_v[:, q, rp * 512 : (rp + 1) * 512], in_=osb[:])
+
+        g01 = [(q, rp) for q in (0, 1) for rp in (0, 1)]
+        g23 = [(q, rp) for q in (2, 3) for rp in (0, 1)]
+
+        def sweep(groups, k):
+            for g in groups:
+                stage2(g[0], g[1], k, k == 0, k == 7)
+
+        with tc.manual_schedule(engines={mybir.EngineType.PE}):
+            burst(N_WARM, dummy[:, 0:P], dummy[:])
+            for t in range(4):
+                w_tiles(t)
+                load_w1(t)
+            x_prep()
+            for t in range(4):
+                w_quant(t)
+            c_run(0)
+            c_run(1)
+            stage1(0)
+            stage1(1)
+            versions(0, (0, 1, 2, 3))
+            c_run(2)
+            versions(1, (0, 1, 2, 3))
+            stage1(2)
+            stage1(3)
+            versions(2, (0, 1, 2, 3))
+            c_run(3)
+            versions(3, (0, 1, 2, 3))
+            for g in g01:
+                open_group(g[0], g[1])
+            sweep(g01, 0)
+            sweep(g01, 1)
+            stage1(4)
+            stage1(5)
+            versions(4, (0, 1, 2, 3))
+            sweep(g01, 2)
+            stage1(6)
+            stage1(7)
+            versions(5, (0, 1, 2, 3))
+            sweep(g01, 3)
+            stage1(8)
+            for g in g23:
+                open_group(g[0], g[1])
+            for k in range(4):
+                sweep(g23, k)
+            versions(8, (0, 1))
+            versions(6, (0, 1))
+            versions(7, (0, 1))
+            sweep(g01 + g23, 4)
+            versions(6, (2, 3))
+            versions(7, (2, 3))
+            sweep(g01 + g23, 5)
+            sweep(g01 + g23, 8)
+            for rp in range(2):
+                for q in range(4):
+                    stage2(q, rp, 6, False, False)
+                    stage2(q, rp, 7, False, True)
+                    finish_group(q, rp)

@@ -128,7 +128,10 @@ def tile_psr4convf_kernel(tc, x, W, W1, out):
             src = wraw[t][:].rearrange("m (a u e k) -> m k u a e", u=2, e=2, k=NK)
             for k0, k1 in ((0, 4), (4, 8)):
                 for u in range(2):
-                    nc.vector.tensor_copy(out=wk[:, k0:k1, u, :, :], in_=src[:, k0:k1, u, :, :])
+                    nc.vector.tensor_copy(
+                        out=wk[:, k0:k1, u, :, :].rearrange("m k a e -> m a k e"),
+                        in_=src[:, k0:k1, u, :, :].rearrange("m k a e -> m a k e"),
+                    )
             for u in range(2):
                 nc.scalar.copy(out=wk[:, 8, u, :, :], in_=src[:, 8, u, :, :])
             wg = stage.tile([P, NK * 512], BF16, name="wg", tag="grouped", align_bytes=64)

@@ -15,11 +15,11 @@ NK = 9
 HW = 256
 ROW = 64
 RING = [(-1, -1), (-1, 0), (-1, 1), (0, 1), (1, 1), (1, 0), (1, -1), (0, -1)]
-NSET = 3
-N_H0 = 5
+NSET = 4
+NHC = 4
 N_WARM = 8
-Z_DT = BF16
 C_TILES = [(0, 2), (2, 2), (4, 2), (6, 2), (8, 1)]
+K_ORDER = [0, 1, 2, 3, 4, 5, 8, 6, 7]
 
 FLOPS = 2 * 2 * NK * 512 * 512 * HW
 
@@ -36,7 +36,7 @@ def tile_psr4convf_kernel(tc, x, W, W1, out):
         raw = ctx.enter_context(tc.tile_pool(name="raw", bufs=4))
         regr = ctx.enter_context(tc.tile_pool(name="regr", bufs=2))
         stage = ctx.enter_context(tc.tile_pool(name="stage", bufs=5))
-        outp = ctx.enter_context(tc.tile_pool(name="outp", bufs=4))
+        outp = ctx.enter_context(tc.tile_pool(name="outp", bufs=8))
         work = ctx.enter_context(tc.psum_pool(name="work", bufs=8))
 
         wraw = []
@@ -57,22 +57,15 @@ def tile_psr4convf_kernel(tc, x, W, W1, out):
         nc.vector.memset(dummy[:], 0.0)
         ident_f = const.tile([P, P], F32, name="ident_f")
         make_identity(nc, ident_f[:])
-        h0s = []
-        for k in range(N_H0):
-            h0k = const.tile([P, 18, 16, 4], BF16, name="h0_%d" % k, align_bytes=64)
-            nc.vector.memset(h0k[:, 0:18:17, :, :], 0.0)
-            h0s.append(h0k)
-        hset = []
-        for s in range(NSET):
-            pair = []
-            for nm in ("hp", "hm"):
-                ht = const.tile([P, 18, 16, 4], BF16, name="%s_%d" % (nm, s), align_bytes=64)
-                nc.vector.memset(ht[:], 0.0)
-                pair.append(ht)
-            hset.append(pair)
         warm = const.tile([P, 1], F32, name="warm")
         nc.vector.memset(warm[:], 0.0)
         nc.scalar.activation(out=warm[:], in_=warm[:], func=RELU)
+        h0all = const.tile([P, NK, 18, 16, 4], BF16, name="h0all", align_bytes=64)
+        nc.vector.memset(h0all[:, :, 0:18:17, :, :], 0.0)
+        hxall = const.tile([P, 2 * NSET, 18, 16, 4], BF16, name="hxall", align_bytes=64)
+        nc.vector.memset(hxall[:, :, 0:18:17, :, :], 0.0)
+        nc.vector.memset(hxall[:, 0 : 2 * NSET : 2, 1:17, 14:16, :], 0.0)
+        nc.vector.memset(hxall[:, 1 : 2 * NSET : 2, 1:17, 0:2, :], 0.0)
 
         xg = const.tile([P, HW, 4], BF16, name="xg", align_bytes=64)
         xc = const.tile([P, HW], U32, name="xc", align_bytes=64)
@@ -81,14 +74,13 @@ def tile_psr4convf_kernel(tc, x, W, W1, out):
         ws = const.tile([P, 4 * NK * P], U8, name="ws", align_bytes=64)
         w1c = const.tile([P, 4 * NK * P], U32, name="w1c", align_bytes=64)
         w1s = const.tile([P, 4 * NK * P], U8, name="w1s", align_bytes=64)
-        hc = []
-        hs = []
-        for k in range(NK):
-            nver = 4 if k < 8 else 2
-            hck = const.tile([P, nver * HW], U32, name="hc%d" % k, align_bytes=64)
-            hsk = const.tile([P, nver * HW], U8, name="hs%d" % k, align_bytes=64)
-            hc.append(hck)
-            hs.append(hsk)
+        hc_t = []
+        hs_t = []
+        for i in range(NHC):
+            hck = const.tile([P, 4 * HW], U32, name="hc%d" % i, align_bytes=64)
+            hsk = const.tile([P, 4 * HW], U8, name="hs%d" % i, align_bytes=64)
+            hc_t.append(hck)
+            hs_t.append(hsk)
 
         def x_prep():
             nc.vector.tensor_copy(out=xg[:], in_=xraw[:].rearrange("p j n -> p n j"))
@@ -108,8 +100,6 @@ def tile_psr4convf_kernel(tc, x, W, W1, out):
             for i in range(n):
                 nc.tensor.matmul(out=wps[:], lhsT=lhs, rhs=rhs, start=True, stop=True)
 
-        wgs = {}
-
         def transposed(words, grouped):
             for k0, nk in C_TILES:
                 tp1 = work.tile([P, 2, 2, P], F32, name="tp1", tag="bank")
@@ -122,6 +112,9 @@ def tile_psr4convf_kernel(tc, x, W, W1, out):
                     .rearrange("p (k m u) -> p k m u", k=nk, u=2)
                 )
                 nc.scalar.copy(out=dst, in_=tp1[:, 0:nk, :, :].rearrange("p k u m -> p k m u"))
+
+        wgs = {}
+        w1gs = {}
 
         def w_tiles(t):
             wk = regr.tile([P, NK, 2, P, 2], BF16, name="wk", tag="wk")
@@ -139,67 +132,63 @@ def tile_psr4convf_kernel(tc, x, W, W1, out):
             words = wk[:].rearrange("m k u a e -> m (k u a e)").bitcast(F32).rearrange("m (k u a) -> m k u a", k=NK, u=2)
             transposed(words, wg)
 
-        def w_quant(t):
-            quantize_piece(wgs[t], wc, ws, t, 0, 4)
-            quantize_piece(wgs[t], wc, ws, t, 4, 8)
-            quantize_piece(wgs[t], wc, ws, t, 8, 9)
+        def w_quant(t, k0, k1):
+            quantize_piece(wgs[t], wc, ws, t, k0, k1)
 
         def c_run(q):
             w1g = stage.tile([P, NK * 512], BF16, name="w1g", tag="grouped", align_bytes=64)
+            w1gs[q] = w1g
             words = w1raw[q][:].bitcast(F32).rearrange("m (k a u) -> m k u a", k=NK, u=2)
-            for k0, nk in C_TILES:
-                tp1 = work.tile([P, 2, 2, P], F32, name="tp1", tag="bank")
-                for kk in range(nk):
-                    for u in range(2):
-                        nc.tensor.transpose(out=tp1[:, kk, u, :], in_=words[:, k0 + kk, u, :], identity=ident_f[:])
-                dst = (
-                    w1g[:, k0 * 512 : (k0 + nk) * 512]
-                    .bitcast(F32)
-                    .rearrange("p (k m u) -> p k m u", k=nk, u=2)
-                )
-                nc.scalar.copy(out=dst, in_=tp1[:, 0:nk, :, :].rearrange("p k u m -> p k m u"))
-                if k0 == 2:
-                    quantize_piece(w1g, w1c, w1s, q, 0, 4)
-                if k0 == 6:
-                    quantize_piece(w1g, w1c, w1s, q, 4, 8)
-            quantize_piece(w1g, w1c, w1s, q, 8, 9)
+            transposed(words, w1g)
 
-        set_of = {}
+        def c_quant(q, k0, k1):
+            quantize_piece(w1gs[q], w1c, w1s, q, k0, k1)
 
         def stage1(k):
-            set_of[k] = hset[k % NSET]
-            h0 = h0s[k % N_H0]
-            hp, hm = set_of[k]
-            h0f = h0[:].rearrange("p a b t -> p (a b t)")
-            for nh in range(2):
-                z = work.tile([P, 4, P], Z_DT, name="z", tag="bank")
-                for t in range(4):
-                    c0 = (t * NK + k) * P
-                    nc.tensor.matmul_mx(
-                        out=z[:, t, :],
-                        lhsT=wc[:, c0 : c0 + P].bitcast(FP8X4),
-                        lhsT_scale=ws[:, c0 : c0 + P],
-                        rhs=xc[:, nh * P : (nh + 1) * P].bitcast(FP8X4),
-                        rhs_scale=xs[:, nh * P : (nh + 1) * P],
-                        start=True,
-                        stop=True,
-                    )
-                nc.scalar.activation(
-                    out=h0f[:, ROW + nh * 512 : ROW + (nh + 1) * 512].rearrange("p (n t) -> p n t", t=4),
-                    in_=z[:].rearrange("p t n -> p n t"),
-                    func=RELU,
+            z = work.tile([P, 4, HW], BF16, name="z", tag="bank")
+            for t in range(4):
+                c0 = (t * NK + k) * P
+                nc.tensor.matmul_mx(
+                    out=z[:, t, :],
+                    lhsT=wc[:, c0 : c0 + P].bitcast(FP8X4),
+                    lhsT_scale=ws[:, c0 : c0 + P],
+                    rhs=xc[:].bitcast(FP8X4),
+                    rhs_scale=xs[:],
+                    start=True,
+                    stop=True,
                 )
-            if k < 8:
-                nc.vector.tensor_copy(out=hp[:, 1:17, 0:15, :], in_=h0[:, 1:17, 1:16, :])
-                nc.vector.tensor_copy(out=hm[:, 1:17, 1:16, :], in_=h0[:, 1:17, 0:15, :])
+            dst = h0all[:, k, 1:17, :, :].rearrange("p a b t -> p (a b) t")
+            if k % 2 == 1:
+                nc.vector.tensor_scalar_max(out=dst, in0=z[:].rearrange("p t n -> p n t"), scalar1=0.0)
+            else:
+                nc.scalar.activation(out=dst, in_=z[:].rearrange("p t n -> p n t"), func=RELU)
 
-        def versions(k, which):
-            h0 = h0s[k % N_H0]
-            hp, hm = set_of[k]
-            by_dx = {0: h0, 1: hp, -1: hm}
-            for v in which:
+        ring_order = [k for k in K_ORDER if k < 8]
+        slot_of = {}
+
+        def shift_upto(n):
+            while len(slot_of) < min(n, 8):
+                k = ring_order[len(slot_of)]
+                s = len(slot_of) % NSET
+                slot_of[k] = s
+                nc.sync.dma_start(out=hxall[:, 2 * s, 1:17, 0:15, :], in_=h0all[:, k, 1:17, 1:16, :])
+                nc.sync.dma_start(out=hxall[:, 2 * s + 1, 1:17, 1:16, :], in_=h0all[:, k, 1:17, 0:15, :])
+
+        hc = {}
+        hs = {}
+
+        def versions(k):
+            hs[k] = hs_t[len(hc) % NHC]
+            hc[k] = hc_t[len(hc) % NHC]
+            for v in range(4 if k < 8 else 2):
                 dy, dx = RING[(k + 2 * v) % 8] if k < 8 else (0, 0)
-                flat = by_dx[dx][:].rearrange("p a b t -> p (a b t)")
+                if dx == 0:
+                    image = h0all[:, k]
+                elif dx == 1:
+                    image = hxall[:, 2 * slot_of[k]]
+                else:
+                    image = hxall[:, 2 * slot_of[k] + 1]
+                flat = image.rearrange("p a b t -> p (a b t)")
                 nc.vector.quantize_mx(
                     out=hc[k][:, v * HW : (v + 1) * HW].bitcast(FP8X4),
                     scales=hs[k][:, v * HW : (v + 1) * HW],
@@ -207,12 +196,14 @@ def tile_psr4convf_kernel(tc, x, W, W1, out):
                 )
 
         accs = {}
+        passes = {}
 
-        def open_group(q, rp):
-            acc = work.tile([P, 512], F32, name="acc", tag="bank")
-            accs[(q, rp)] = acc
-
-        def stage2(q, rp, k, first_pass, last_pass):
+        def stage2(q, rp, k):
+            if (q, rp) not in accs:
+                acc = work.tile([P, 512], F32, name="acc", tag="bank")
+                accs[(q, rp)] = acc
+                passes[(q, rp)] = 0
+            passes[(q, rp)] += 1
             c0 = (q * NK + k) * P
             r0 = rp * 512 if k < 8 else 0
             nc.tensor.matmul_mx(
@@ -221,8 +212,8 @@ def tile_psr4convf_kernel(tc, x, W, W1, out):
                 lhsT_scale=w1s[:, c0 : c0 + P],
                 rhs=hc[k][:, r0 : r0 + 512].bitcast(FP8X4),
                 rhs_scale=hs[k][:, r0 : r0 + 512],
-                start=first_pass,
-                stop=last_pass,
+                start=passes[(q, rp)] == 1,
+                stop=passes[(q, rp)] == NK,
             )
 
         def finish_group(q, rp):
@@ -233,12 +224,11 @@ def tile_psr4convf_kernel(tc, x, W, W1, out):
                 nc.scalar.copy(out=osb[:], in_=accs[(q, rp)][:])
             nc.sync.dma_start(out=out_v[:, q, rp * 512 : (rp + 1) * 512], in_=osb[:])
 
-        g01 = [(q, rp) for q in (0, 1) for rp in (0, 1)]
-        g23 = [(q, rp) for q in (2, 3) for rp in (0, 1)]
+        groups = [(q, rp) for q in range(4) for rp in range(2)]
 
-        def sweep(groups, k):
-            for g in groups:
-                stage2(g[0], g[1], k, k == 0, k == 7)
+        def sweep(k):
+            for q, rp in groups:
+                stage2(q, rp, k)
 
         with tc.manual_schedule(engines={mybir.EngineType.PE}):
             burst(N_WARM, dummy[:, 0:P], dummy[:])
@@ -247,46 +237,41 @@ def tile_psr4convf_kernel(tc, x, W, W1, out):
                 load_w1(t)
             x_prep()
             for t in range(4):
-                w_quant(t)
+                w_quant(t, 0, 4)
             c_run(0)
+            for k in range(0, 4):
+                stage1(k)
+            shift_upto(NSET)
+            for t in range(4):
+                w_quant(t, 4, 8)
+                w_quant(t, 8, 9)
             c_run(1)
-            stage1(0)
-            stage1(1)
-            versions(0, (0, 1, 2, 3))
+            for k in range(4, 8):
+                stage1(k)
+            c_quant(0, 0, 4)
+            c_quant(1, 0, 4)
+            versions(K_ORDER[0])
+            shift_upto(NSET + 1)
             c_run(2)
-            versions(1, (0, 1, 2, 3))
-            stage1(2)
-            stage1(3)
-            versions(2, (0, 1, 2, 3))
-            c_run(3)
-            versions(3, (0, 1, 2, 3))
-            for g in g01:
-                open_group(g[0], g[1])
-            sweep(g01, 0)
-            sweep(g01, 1)
-            stage1(4)
-            stage1(5)
-            versions(4, (0, 1, 2, 3))
-            sweep(g01, 2)
-            stage1(6)
-            stage1(7)
-            versions(5, (0, 1, 2, 3))
-            sweep(g01, 3)
             stage1(8)
-            for g in g23:
-                open_group(g[0], g[1])
-            for k in range(4):
-                sweep(g23, k)
-            versions(8, (0, 1))
-            versions(6, (0, 1))
-            versions(7, (0, 1))
-            sweep(g01 + g23, 4)
-            versions(6, (2, 3))
-            versions(7, (2, 3))
-            sweep(g01 + g23, 5)
-            sweep(g01 + g23, 8)
+            c_run(3)
+            c_quant(2, 0, 4)
+            c_quant(3, 0, 4)
+            for i, k in enumerate(K_ORDER[0:7]):
+                if i > 0:
+                    if k == 4:
+                        for q in range(4):
+                            c_quant(q, 4, 8)
+                    if k == 8:
+                        for q in range(4):
+                            c_quant(q, 8, 9)
+                    versions(k)
+                    shift_upto(NSET + 1 + i)
+                sweep(k)
+            versions(K_ORDER[7])
+            versions(K_ORDER[8])
             for rp in range(2):
                 for q in range(4):
-                    stage2(q, rp, 6, False, False)
-                    stage2(q, rp, 7, False, True)
+                    stage2(q, rp, K_ORDER[7])
+                    stage2(q, rp, K_ORDER[8])
                     finish_group(q, rp)

@@ -64,8 +64,8 @@ def tile_psr4convf_kernel(tc, x, W, W1, out):
         nc.vector.memset(h0all[:, :, 0:18:17, :, :], 0.0)
         hxall = const.tile([P, 2 * NSET, 18, 16, 4], BF16, name="hxall", align_bytes=64)
         nc.vector.memset(hxall[:, :, 0:18:17, :, :], 0.0)
-        nc.vector.memset(hxall[:, 0 : 2 * NSET : 2, 1:17, 14:16, :], 0.0)
-        nc.vector.memset(hxall[:, 1 : 2 * NSET : 2, 1:17, 0:2, :], 0.0)
+        zeros = const.tile([P, 16, 4], BF16, name="zeros")
+        nc.vector.memset(zeros[:], 0.0)
 
         xg = const.tile([P, HW, 4], BF16, name="xg", align_bytes=64)
         xc = const.tile([P, HW], U32, name="xc", align_bytes=64)
@@ -171,8 +171,13 @@ def tile_psr4convf_kernel(tc, x, W, W1, out):
                 k = ring_order[len(slot_of)]
                 s = len(slot_of) % NSET
                 slot_of[k] = s
-                nc.sync.dma_start(out=hxall[:, 2 * s, 1:17, 0:15, :], in_=h0all[:, k, 1:17, 1:16, :])
-                nc.sync.dma_start(out=hxall[:, 2 * s + 1, 1:17, 1:16, :], in_=h0all[:, k, 1:17, 0:15, :])
+                flat = h0all[:, k].rearrange("p a b t -> p (a b t)")
+                plus = hxall[:, 2 * s].rearrange("p a b t -> p (a b t)")
+                minus = hxall[:, 2 * s + 1].rearrange("p a b t -> p (a b t)")
+                nc.sync.dma_start(out=plus[:, ROW : ROW + 4 * HW - 4], in_=flat[:, ROW + 4 : ROW + 4 * HW])
+                nc.sync.dma_start(out=minus[:, ROW + 4 : ROW + 4 * HW], in_=flat[:, ROW : ROW + 4 * HW - 4])
+                nc.scalar.copy(out=hxall[:, 2 * s, 1:17, 15, :], in_=zeros[:])
+                nc.scalar.copy(out=hxall[:, 2 * s + 1, 1:17, 0, :], in_=zeros[:])
 
         hc = {}
         hs = {}

@@ -18,6 +18,7 @@ RING = [(-1, -1), (-1, 0), (-1, 1), (0, 1), (1, 1), (1, 0), (1, -1), (0, -1)]
 NSET = 4
 NHC = 4
 N_WARM = 8
+LATE = 3
 C_TILES = [(0, 2), (2, 2), (4, 2), (6, 2), (8, 1)]
 K_ORDER = [0, 1, 2, 3, 4, 5, 8, 6, 7]
 
@@ -119,14 +120,12 @@ def tile_psr4convf_kernel(tc, x, W, W1, out):
         def w_tiles(t):
             wk = regr.tile([P, NK, 2, P, 2], BF16, name="wk", tag="wk")
             src = wraw[t][:].rearrange("m (a u e k) -> m k u a e", u=2, e=2, k=NK)
-            for k0, k1 in ((0, 4), (4, 8)):
+            for k0, k1 in ((0, 3), (3, 6), (6, 9)):
                 for u in range(2):
                     nc.vector.tensor_copy(
                         out=wk[:, k0:k1, u, :, :].rearrange("m k a e -> m a k e"),
                         in_=src[:, k0:k1, u, :, :].rearrange("m k a e -> m a k e"),
                     )
-            for u in range(2):
-                nc.scalar.copy(out=wk[:, 8, u, :, :], in_=src[:, 8, u, :, :])
             wg = stage.tile([P, NK * 512], BF16, name="wg", tag="grouped", align_bytes=64)
             wgs[t] = wg
             words = wk[:].rearrange("m k u a e -> m (k u a e)").bitcast(F32).rearrange("m (k u a) -> m k u a", k=NK, u=2)
@@ -231,8 +230,8 @@ def tile_psr4convf_kernel(tc, x, W, W1, out):
 
         groups = [(q, rp) for q in range(4) for rp in range(2)]
 
-        def sweep(k):
-            for q, rp in groups:
+        def sweep(k, some):
+            for q, rp in some:
                 stage2(q, rp, k)
 
         with tc.manual_schedule(engines={mybir.EngineType.PE}):
@@ -261,7 +260,6 @@ def tile_psr4convf_kernel(tc, x, W, W1, out):
             stage1(8)
             c_run(3)
             c_quant(2, 0, 4)
-            c_quant(3, 0, 4)
             for i, k in enumerate(K_ORDER[0:7]):
                 if i > 0:
                     if k == 4:
@@ -272,7 +270,15 @@ def tile_psr4convf_kernel(tc, x, W, W1, out):
                             c_quant(q, 8, 9)
                     versions(k)
                     shift_upto(NSET + 1 + i)
-                sweep(k)
+                if i == 1:
+                    c_quant(3, 0, 4)
+                if i < LATE:
+                    sweep(k, groups[0:6])
+                    if i == LATE - 1:
+                        for kk in K_ORDER[0:LATE]:
+                            sweep(kk, groups[6:8])
+                else:
+                    sweep(k, groups)
             versions(K_ORDER[7])
             versions(K_ORDER[8])
             for rp in range(2):

@@ -19,6 +19,7 @@ NSET = 4
 NHC = 4
 N_WARM = 8
 LATE = 3
+LOAD_ORDER = [("W", 0), ("W", 1), ("W1", 0), ("W", 2), ("W1", 1), ("W", 3), ("x", 0), ("W1", 2), ("W1", 3)]
 C_TILES = [(0, 2), (2, 2), (4, 2), (6, 2), (8, 1)]
 K_ORDER = [0, 1, 2, 3, 4, 5, 8, 6, 7]
 
@@ -36,23 +37,23 @@ def tile_psr4convf_kernel(tc, x, W, W1, out):
         const = ctx.enter_context(tc.tile_pool(name="const", bufs=1))
         raw = ctx.enter_context(tc.tile_pool(name="raw", bufs=4))
         regr = ctx.enter_context(tc.tile_pool(name="regr", bufs=2))
-        stage = ctx.enter_context(tc.tile_pool(name="stage", bufs=5))
-        outp = ctx.enter_context(tc.tile_pool(name="outp", bufs=8))
+        stage = ctx.enter_context(tc.tile_pool(name="stage", bufs=6))
         work = ctx.enter_context(tc.psum_pool(name="work", bufs=8))
 
-        wraw = []
-        for t in range(4):
-            r = raw.tile([P, NK * 512], BF16, name="wraw%d" % t, tag="raw")
-            nc.sync.dma_start(out=r[:], in_=w_v[:, t, :])
-            wraw.append(r)
+        wraw = {}
+        w1raw = {}
         xraw = const.tile([P, 4, HW], BF16, name="xraw")
-        nc.sync.dma_start(out=xraw[:], in_=x_v)
-        w1raw = []
-
-        def load_w1(q):
-            r1 = raw.tile([P, NK * 512], BF16, name="w1raw%d" % q, tag="raw")
-            nc.sync.dma_start(out=r1[:], in_=w1_v[:, q, :])
-            w1raw.append(r1)
+        for kind, i in LOAD_ORDER:
+            if kind == "W":
+                r = raw.tile([P, NK * 512], BF16, name="wraw%d" % i, tag="raw")
+                nc.sync.dma_start(out=r[:], in_=w_v[:, i, :])
+                wraw[i] = r
+            elif kind == "W1":
+                r1 = raw.tile([P, NK * 512], BF16, name="w1raw%d" % i, tag="raw")
+                nc.sync.dma_start(out=r1[:], in_=w1_v[:, i, :])
+                w1raw[i] = r1
+            else:
+                nc.sync.dma_start(out=xraw[:], in_=x_v)
 
         dummy = const.tile([P, 512], BF16, name="dummy")
         nc.vector.memset(dummy[:], 0.0)
@@ -220,13 +221,18 @@ def tile_psr4convf_kernel(tc, x, W, W1, out):
                 stop=passes[(q, rp)] == NK,
             )
 
+        osbs = {}
+
         def finish_group(q, rp):
-            osb = outp.tile([P, 512], F32, name="osb", tag="osb")
+            if rp not in osbs:
+                osb4 = raw.tile([P, 4, 512], F32, name="osb4", tag="raw")
+                osbs[rp] = osb4
+            osb = osbs[rp][:, q, :]
             if q % 2 == 0:
-                nc.vector.tensor_copy(out=osb[:], in_=accs[(q, rp)][:])
+                nc.vector.tensor_copy(out=osb, in_=accs[(q, rp)][:])
             else:
-                nc.scalar.copy(out=osb[:], in_=accs[(q, rp)][:])
-            nc.sync.dma_start(out=out_v[:, q, rp * 512 : (rp + 1) * 512], in_=osb[:])
+                nc.scalar.copy(out=osb, in_=accs[(q, rp)][:])
+            nc.sync.dma_start(out=out_v[:, q, rp * 512 : (rp + 1) * 512], in_=osb)
 
         groups = [(q, rp) for q in range(4) for rp in range(2)]
 
@@ -236,27 +242,28 @@ def tile_psr4convf_kernel(tc, x, W, W1, out):
 
         with tc.manual_schedule(engines={mybir.EngineType.PE}):
             burst(N_WARM, dummy[:, 0:P], dummy[:])
-            for t in range(4):
-                w_tiles(t)
-                load_w1(t)
+            w_tiles(0)
+            w_tiles(1)
+            c_run(0)
+            w_tiles(2)
+            c_run(1)
+            w_tiles(3)
+            c_run(2)
             x_prep()
             for t in range(4):
                 w_quant(t, 0, 4)
-            c_run(0)
             for k in range(0, 4):
                 stage1(k)
             shift_upto(NSET)
             for t in range(4):
                 w_quant(t, 4, 8)
                 w_quant(t, 8, 9)
-            c_run(1)
             for k in range(4, 8):
                 stage1(k)
             c_quant(0, 0, 4)
             c_quant(1, 0, 4)
             versions(K_ORDER[0])
             shift_upto(NSET + 1)
-            c_run(2)
             stage1(8)
             c_run(3)
             c_quant(2, 0, 4)

@@ -66,8 +66,6 @@ def tile_psr4convf_kernel(tc, x, W, W1, out):
         nc.vector.memset(h0all[:, :, 0:18:17, :, :], 0.0)
         hxall = const.tile([P, 2 * NSET, 18, 16, 4], BF16, name="hxall", align_bytes=64)
         nc.vector.memset(hxall[:, :, 0:18:17, :, :], 0.0)
-        zeros = const.tile([P, 16, 4], BF16, name="zeros")
-        nc.vector.memset(zeros[:], 0.0)
 
         xg = const.tile([P, HW, 4], BF16, name="xg", align_bytes=64)
         xc = const.tile([P, HW], U32, name="xc", align_bytes=64)
@@ -176,8 +174,8 @@ def tile_psr4convf_kernel(tc, x, W, W1, out):
                 minus = hxall[:, 2 * s + 1].rearrange("p a b t -> p (a b t)")
                 nc.sync.dma_start(out=plus[:, ROW : ROW + 4 * HW - 4], in_=flat[:, ROW + 4 : ROW + 4 * HW])
                 nc.sync.dma_start(out=minus[:, ROW + 4 : ROW + 4 * HW], in_=flat[:, ROW : ROW + 4 * HW - 4])
-                nc.scalar.copy(out=hxall[:, 2 * s, 1:17, 15, :], in_=zeros[:])
-                nc.scalar.copy(out=hxall[:, 2 * s + 1, 1:17, 0, :], in_=zeros[:])
+                nc.gpsimd.memset(hxall[:, 2 * s, 1:17, 15, :], 0.0)
+                nc.gpsimd.memset(hxall[:, 2 * s + 1, 1:17, 0, :], 0.0)
 
         hc = {}
         hs = {}

@@ -21,7 +21,7 @@ N_WARM = 8
 LATE = 3
 LOAD_ORDER = [("W", 0), ("W", 1), ("W1", 0), ("W", 2), ("W1", 1), ("W", 3), ("x", 0), ("W1", 2), ("W1", 3)]
 C_TILES = [(0, 2), (2, 2), (4, 2), (6, 2), (8, 1)]
-K_ORDER = [0, 1, 2, 3, 4, 5, 8, 6, 7]
+K_ORDER = [0, 1, 2, 3, 4, 5, 6, 7]
 
 FLOPS = 2 * 2 * NK * 512 * 512 * HW
 
@@ -81,6 +81,10 @@ def tile_psr4convf_kernel(tc, x, W, W1, out):
             hsk = const.tile([P, 4 * HW], U8, name="hs%d" % i, align_bytes=64)
             hc_t.append(hck)
             hs_t.append(hsk)
+
+        hc8 = const.tile([P, HW], U32, name="hc8", align_bytes=64)
+        hs8 = const.tile([P, HW], U8, name="hs8", align_bytes=64)
+        u8sb = const.tile([P, 4, HW], F32, name="u8sb")
 
         def x_prep():
             nc.vector.tensor_copy(out=xg[:], in_=xraw[:].rearrange("p j n -> p n j"))
@@ -183,8 +187,8 @@ def tile_psr4convf_kernel(tc, x, W, W1, out):
         def versions(k):
             hs[k] = hs_t[len(hc) % NHC]
             hc[k] = hc_t[len(hc) % NHC]
-            for v in range(4 if k < 8 else 2):
-                dy, dx = RING[(k + 2 * v) % 8] if k < 8 else (0, 0)
+            for v in range(4):
+                dy, dx = RING[(k + 2 * v) % 8]
                 if dx == 0:
                     image = h0all[:, k]
                 elif dx == 1:
@@ -198,6 +202,29 @@ def tile_psr4convf_kernel(tc, x, W, W1, out):
                     in_=flat[:, (1 + dy) * ROW : (1 + dy) * ROW + 4 * HW],
                 )
 
+        def centre_quant():
+            nc.vector.quantize_mx(
+                out=hc8[:].bitcast(FP8X4),
+                scales=hs8[:],
+                in_=h0all[:, 8].rearrange("p a b t -> p (a b t)")[:, ROW : ROW + 4 * HW],
+            )
+
+        def centre():
+            for i in range(2):
+                c8 = work.tile([P, 2, HW], F32, name="c8", tag="bank")
+                for j in range(2):
+                    c0 = ((2 * i + j) * NK + 8) * P
+                    nc.tensor.matmul_mx(
+                        out=c8[:, j, :],
+                        lhsT=w1c[:, c0 : c0 + P].bitcast(FP8X4),
+                        lhsT_scale=w1s[:, c0 : c0 + P],
+                        rhs=hc8[:].bitcast(FP8X4),
+                        rhs_scale=hs8[:],
+                        start=True,
+                        stop=True,
+                    )
+                nc.scalar.copy(out=u8sb[:, 2 * i : 2 * i + 2, :], in_=c8[:])
+
         accs = {}
         passes = {}
 
@@ -208,7 +235,7 @@ def tile_psr4convf_kernel(tc, x, W, W1, out):
                 passes[(q, rp)] = 0
             passes[(q, rp)] += 1
             c0 = (q * NK + k) * P
-            r0 = rp * 512 if k < 8 else 0
+            r0 = rp * 512
             nc.tensor.matmul_mx(
                 out=accs[(q, rp)][:],
                 lhsT=w1c[:, c0 : c0 + P].bitcast(FP8X4),
@@ -216,7 +243,7 @@ def tile_psr4convf_kernel(tc, x, W, W1, out):
                 rhs=hc[k][:, r0 : r0 + 512].bitcast(FP8X4),
                 rhs_scale=hs[k][:, r0 : r0 + 512],
                 start=passes[(q, rp)] == 1,
-                stop=passes[(q, rp)] == NK,
+                stop=passes[(q, rp)] == NK - 1,
             )
 
         osbs = {}
@@ -226,10 +253,12 @@ def tile_psr4convf_kernel(tc, x, W, W1, out):
                 osb4 = raw.tile([P, 4, 512], F32, name="osb4", tag="raw")
                 osbs[rp] = osb4
             osb = osbs[rp][:, q, :]
-            if q % 2 == 0:
-                nc.vector.tensor_copy(out=osb, in_=accs[(q, rp)][:])
-            else:
-                nc.scalar.copy(out=osb, in_=accs[(q, rp)][:])
+            nc.vector.tensor_tensor(
+                out=osb.rearrange("p (r n) -> p r n", r=2),
+                in0=accs[(q, rp)][:].rearrange("p (r n) -> p r n", r=2),
+                in1=u8sb[:, q : q + 1, :].to_broadcast([P, 2, HW]),
+                op=mybir.AluOpType.add,
+            )
             nc.sync.dma_start(out=out_v[:, q, rp * 512 : (rp + 1) * 512], in_=osb)
 
         groups = [(q, rp) for q in range(4) for rp in range(2)]
@@ -254,40 +283,42 @@ def tile_psr4convf_kernel(tc, x, W, W1, out):
                 stage1(k)
             shift_upto(NSET)
             for t in range(4):
-                w_quant(t, 4, 8)
                 w_quant(t, 8, 9)
+                w_quant(t, 4, 8)
+            stage1(8)
             for k in range(4, 8):
                 stage1(k)
             c_quant(0, 0, 4)
             c_quant(1, 0, 4)
             versions(K_ORDER[0])
             shift_upto(NSET + 1)
-            stage1(8)
             c_run(3)
             c_quant(2, 0, 4)
-            for i, k in enumerate(K_ORDER[0:7]):
+            centre_quant()
+            for q in range(4):
+                c_quant(q, 8, 9)
+            for i, k in enumerate(K_ORDER[0:6]):
                 if i > 0:
                     if k == 4:
                         for q in range(4):
                             c_quant(q, 4, 8)
-                    if k == 8:
-                        for q in range(4):
-                            c_quant(q, 8, 9)
                     versions(k)
                     shift_upto(NSET + 1 + i)
                 if i == 1:
                     c_quant(3, 0, 4)
                 if i < LATE:
                     sweep(k, groups[0:6])
+                    if i == LATE - 2:
+                        centre()
                     if i == LATE - 1:
                         for kk in K_ORDER[0:LATE]:
                             sweep(kk, groups[6:8])
                 else:
                     sweep(k, groups)
+            versions(K_ORDER[6])
             versions(K_ORDER[7])
-            versions(K_ORDER[8])
             for rp in range(2):
                 for q in range(4):
+                    stage2(q, rp, K_ORDER[6])
                     stage2(q, rp, K_ORDER[7])
-                    stage2(q, rp, K_ORDER[8])
                     finish_group(q, rp)

@@ -125,10 +125,11 @@ def tile_psr4convf_kernel(tc, x, W, W1, out):
             src = wraw[t][:].rearrange("m (a u e k) -> m k u a e", u=2, e=2, k=NK)
             for k0, k1 in ((0, 3), (3, 6), (6, 9)):
                 for u in range(2):
-                    nc.vector.tensor_copy(
-                        out=wk[:, k0:k1, u, :, :].rearrange("m k a e -> m a k e"),
-                        in_=src[:, k0:k1, u, :, :].rearrange("m k a e -> m a k e"),
-                    )
+                    dst = wk[:, k0:k1, u, :, :].rearrange("m k a e -> m a k e")
+                    if t == 0 and k0 == 6:
+                        nc.scalar.copy(out=dst, in_=src[:, k0:k1, u, :, :].rearrange("m k a e -> m a k e"))
+                    else:
+                        nc.vector.tensor_copy(out=dst, in_=src[:, k0:k1, u, :, :].rearrange("m k a e -> m a k e"))
             wg = stage.tile([P, NK * 512], BF16, name="wg", tag="grouped", align_bytes=64)
             wgs[t] = wg
             words = wk[:].rearrange("m k u a e -> m (k u a e)").bitcast(F32).rearrange("m (k u a) -> m k u a", k=NK, u=2)
@@ -173,6 +174,12 @@ def tile_psr4convf_kernel(tc, x, W, W1, out):
                 k = ring_order[len(slot_of)]
                 s = len(slot_of) % NSET
                 slot_of[k] = s
+                if len(slot_of) == 1:
+                    nc.gpsimd.memset(hxall[:, 2 * s, 1:17, 14:16, :], 0.0)
+                    nc.gpsimd.memset(hxall[:, 2 * s + 1, 1:17, 0:2, :], 0.0)
+                    nc.vector.tensor_copy(out=hxall[:, 2 * s, 1:17, 0:15, :], in_=h0all[:, k, 1:17, 1:16, :])
+                    nc.vector.tensor_copy(out=hxall[:, 2 * s + 1, 1:17, 1:16, :], in_=h0all[:, k, 1:17, 0:15, :])
+                    continue
                 flat = h0all[:, k].rearrange("p a b t -> p (a b t)")
                 plus = hxall[:, 2 * s].rearrange("p a b t -> p (a b t)")
                 minus = hxall[:, 2 * s + 1].rearrange("p a b t -> p (a b t)")

@@ -147,8 +147,11 @@ def tile_psr4convf_kernel(tc, x, W, W1, out):
         def c_quant(q, k0, k1):
             quantize_piece(w1gs[q], w1c, w1s, q, k0, k1)
 
-        def stage1(k):
+        zs = {}
+
+        def stage1_passes(k):
             z = work.tile([P, 4, HW], BF16, name="z", tag="bank")
+            zs[k] = z
             for t in range(4):
                 c0 = (t * NK + k) * P
                 nc.tensor.matmul_mx(
@@ -160,11 +163,18 @@ def tile_psr4convf_kernel(tc, x, W, W1, out):
                     start=True,
                     stop=True,
                 )
+
+        def stage1_relu(k):
+            z = zs[k]
             dst = h0all[:, k, 1:17, :, :].rearrange("p a b t -> p (a b) t")
-            if k % 2 == 1:
+            if k in (1, 3, 5):
                 nc.vector.tensor_scalar_max(out=dst, in0=z[:].rearrange("p t n -> p n t"), scalar1=0.0)
             else:
                 nc.scalar.activation(out=dst, in_=z[:].rearrange("p t n -> p n t"), func=RELU)
+
+        def stage1(k):
+            stage1_passes(k)
+            stage1_relu(k)
 
         ring_order = [k for k in K_ORDER if k < 8]
         slot_of = {}
@@ -293,8 +303,10 @@ def tile_psr4convf_kernel(tc, x, W, W1, out):
                 w_quant(t, 8, 9)
                 w_quant(t, 4, 8)
             stage1(8)
-            for k in range(4, 8):
-                stage1(k)
+            stage1(4)
+            stage1(5)
+            stage1_passes(6)
+            stage1_passes(7)
             c_quant(0, 0, 4)
             c_quant(1, 0, 4)
             versions(K_ORDER[0])
@@ -315,6 +327,9 @@ def tile_psr4convf_kernel(tc, x, W, W1, out):
                     c_quant(3, 0, 4)
                 if i < LATE:
                     sweep(k, groups[0:6])
+                    if i == 0:
+                        stage1_relu(6)
+                        stage1_relu(7)
                     if i == LATE - 2:
                         centre()
                     if i == LATE - 1:

@@ -19,7 +19,7 @@ NSET = 4
 NHC = 4
 N_WARM = 8
 LATE = 3
-LOAD_ORDER = [("W", 0), ("W", 1), ("W1", 0), ("W", 2), ("W1", 1), ("W", 3), ("x", 0), ("W1", 2), ("W1", 3)]
+LOAD_ORDER = [("W", 0), ("W", 1), ("W1", 0), ("W", 2), ("W", 3), ("x", 0), ("W1", 1), ("W1", 2), ("W1", 3)]
 C_TILES = [(0, 2), (2, 2), (4, 2), (6, 2), (8, 1)]
 K_ORDER = [0, 1, 2, 3, 4, 5, 6, 7]
 
@@ -290,8 +290,8 @@ def tile_psr4convf_kernel(tc, x, W, W1, out):
             w_tiles(1)
             c_run(0)
             w_tiles(2)
-            c_run(1)
             w_tiles(3)
+            c_run(1)
             c_run(2)
             x_prep()
             for t in range(4):

@@ -19,7 +19,7 @@ NSET = 4
 NHC = 4
 N_WARM = 8
 LATE = 3
-LOAD_ORDER = [("W", 0), ("W", 1), ("W1", 0), ("W", 2), ("W", 3), ("x", 0), ("W1", 1), ("W1", 2), ("W1", 3)]
+LOAD_ORDER = [("W", 0), ("W", 1), ("W", 2), ("W1", 0), ("W", 3), ("x", 0), ("W1", 1), ("W1", 2), ("W1", 3)]
 C_TILES = [(0, 2), (2, 2), (4, 2), (6, 2), (8, 1)]
 K_ORDER = [0, 1, 2, 3, 4, 5, 6, 7]
 
@@ -288,14 +288,16 @@ def tile_psr4convf_kernel(tc, x, W, W1, out):
             burst(N_WARM, dummy[:, 0:P], dummy[:])
             w_tiles(0)
             w_tiles(1)
-            c_run(0)
             w_tiles(2)
+            c_run(0)
             w_tiles(3)
             c_run(1)
             c_run(2)
             x_prep()
-            for t in range(4):
+            for t in range(3):
                 w_quant(t, 0, 4)
+            w_quant(3, 0, 2)
+            w_quant(3, 2, 4)
             for k in range(0, 4):
                 stage1(k)
             shift_upto(NSET)
@@ -325,8 +327,12 @@ def tile_psr4convf_kernel(tc, x, W, W1, out):
                     shift_upto(NSET + 1 + i)
                 if i == 1:
                     c_quant(3, 0, 4)
-                if i < LATE:
+                if i == 0:
+                    sweep(k, groups[0:6:2])
+                    sweep(k, groups[1:6:2])
+                elif i < LATE:
                     sweep(k, groups[0:6])
+                if i < LATE:
                     if i == 0:
                         stage1_relu(6)
                         stage1_relu(7)

from contextlib import ExitStack

import concourse.mybir as mybir
from concourse.masks import make_identity

F32 = mybir.dt.float32
BF16 = mybir.dt.bfloat16
U32 = mybir.dt.uint32
U8 = mybir.dt.uint8
FP8X4 = mybir.dt.float8_e4m3fn_x4
RELU = mybir.ActivationFunctionType.Relu

P = 128
NK = 9
HW = 256
ROW = 64
RING = [(-1, -1), (-1, 0), (-1, 1), (0, 1), (1, 1), (1, 0), (1, -1), (0, -1)]
NSET = 4
NHC = 4
N_WARM = 8
LATE = 3
LOAD_ORDER = [("W", 0), ("W", 1), ("W", 2), ("W1", 0), ("W", 3), ("x", 0), ("W1", 1), ("W1", 2), ("W1", 3)]
C_TILES = [(0, 2), (2, 2), (4, 2), (6, 2), (8, 1)]
K_ORDER = [0, 1, 2, 3, 4, 5, 6, 7]

FLOPS = 2 * 2 * NK * 512 * 512 * HW


def tile_psr4convf_kernel(tc, x, W, W1, out):
    nc = tc.nc
    x_v = x[0].rearrange("(p j) h w -> p j (h w)", j=4)
    w_v = W.rearrange("(m t) c k -> m t (c k)", t=4)
    w1_v = W1.rearrange("(m q) f -> m q f", q=4)
    out_v = out[0].rearrange("(m q) r h w -> m q (r h w)", q=4)

    with ExitStack() as ctx:
        const = ctx.enter_context(tc.tile_pool(name="const", bufs=1))
        raw = ctx.enter_context(tc.tile_pool(name="raw", bufs=4))
        regr = ctx.enter_context(tc.tile_pool(name="regr", bufs=2))
        stage = ctx.enter_context(tc.tile_pool(name="stage", bufs=6))
        work = ctx.enter_context(tc.psum_pool(name="work", bufs=8))

        wraw = {}
        w1raw = {}
        xraw = const.tile([P, 4, HW], BF16, name="xraw")
        for kind, i in LOAD_ORDER:
            if kind == "W":
                r = raw.tile([P, NK * 512], BF16, name="wraw%d" % i, tag="raw")
                nc.sync.dma_start(out=r[:], in_=w_v[:, i, :])
                wraw[i] = r
            elif kind == "W1":
                r1 = raw.tile([P, NK * 512], BF16, name="w1raw%d" % i, tag="raw")
                nc.sync.dma_start(out=r1[:], in_=w1_v[:, i, :])
                w1raw[i] = r1
            else:
                nc.sync.dma_start(out=xraw[:], in_=x_v)

        dummy = const.tile([P, 512], BF16, name="dummy")
        nc.vector.memset(dummy[:], 0.0)
        ident_f = const.tile([P, P], F32, name="ident_f")
        make_identity(nc, ident_f[:])
        warm = const.tile([P, 1], F32, name="warm")
        nc.vector.memset(warm[:], 0.0)
        nc.scalar.activation(out=warm[:], in_=warm[:], func=RELU)
        h0all = const.tile([P, NK, 18, 16, 4], BF16, name="h0all", align_bytes=64)
        nc.vector.memset(h0all[:, :, 0:18:17, :, :], 0.0)
        hxall = const.tile([P, 2 * NSET, 18, 16, 4], BF16, name="hxall", align_bytes=64)
        nc.vector.memset(hxall[:, :, 0:18:17, :, :], 0.0)

        xg = const.tile([P, HW, 4], BF16, name="xg", align_bytes=64)
        xc = const.tile([P, HW], U32, name="xc", align_bytes=64)
        xs = const.tile([P, HW], U8, name="xs", align_bytes=64)
        wc = const.tile([P, 4 * NK * P], U32, name="wc", align_bytes=64)
        ws = const.tile([P, 4 * NK * P], U8, name="ws", align_bytes=64)
        w1c = const.tile([P, 4 * NK * P], U32, name="w1c", align_bytes=64)
        w1s = const.tile([P, 4 * NK * P], U8, name="w1s", align_bytes=64)
        hc_t = []
        hs_t = []
        for i in range(NHC):
            hck = const.tile([P, 4 * HW], U32, name="hc%d" % i, align_bytes=64)
            hsk = const.tile([P, 4 * HW], U8, name="hs%d" % i, align_bytes=64)
            hc_t.append(hck)
            hs_t.append(hsk)

        hc8 = const.tile([P, HW], U32, name="hc8", align_bytes=64)
        hs8 = const.tile([P, HW], U8, name="hs8", align_bytes=64)
        u8sb = const.tile([P, 4, HW], F32, name="u8sb")

        def x_prep():
            nc.vector.tensor_copy(out=xg[:], in_=xraw[:].rearrange("p j n -> p n j"))
            nc.vector.quantize_mx(out=xc[:].bitcast(FP8X4), scales=xs[:], in_=xg[:].rearrange("p n j -> p (n j)"))

        def quantize_piece(grouped, codes, scales, chunk, k0, k1):
            c0 = (chunk * NK + k0) * P
            c1 = (chunk * NK + k1) * P
            nc.vector.quantize_mx(
                out=codes[:, c0:c1].bitcast(FP8X4),
                scales=scales[:, c0:c1],
                in_=grouped[:, k0 * 512 : k1 * 512],
            )

        def burst(n, lhs, rhs):
            wps = work.tile([P, 512], F32, name="wps", tag="bank")
            for i in range(n):
                nc.tensor.matmul(out=wps[:], lhsT=lhs, rhs=rhs, start=True, stop=True)

        def transposed(words, grouped):
            for k0, nk in C_TILES:
                tp1 = work.tile([P, 2, 2, P], F32, name="tp1", tag="bank")
                for kk in range(nk):
                    for u in range(2):
                        nc.tensor.transpose(out=tp1[:, kk, u, :], in_=words[:, k0 + kk, u, :], identity=ident_f[:])
                dst = (
                    grouped[:, k0 * 512 : (k0 + nk) * 512]
                    .bitcast(F32)
                    .rearrange("p (k m u) -> p k m u", k=nk, u=2)
                )
                nc.scalar.copy(out=dst, in_=tp1[:, 0:nk, :, :].rearrange("p k u m -> p k m u"))

        wgs = {}
        w1gs = {}

        def w_tiles(t):
            wk = regr.tile([P, NK, 2, P, 2], BF16, name="wk", tag="wk")
            src = wraw[t][:].rearrange("m (a u e k) -> m k u a e", u=2, e=2, k=NK)
            for k0, k1 in ((0, 3), (3, 6), (6, 9)):
                for u in range(2):
                    dst = wk[:, k0:k1, u, :, :].rearrange("m k a e -> m a k e")
                    if t == 0 and k0 == 6:
                        nc.scalar.copy(out=dst, in_=src[:, k0:k1, u, :, :].rearrange("m k a e -> m a k e"))
                    else:
                        nc.vector.tensor_copy(out=dst, in_=src[:, k0:k1, u, :, :].rearrange("m k a e -> m a k e"))
            wg = stage.tile([P, NK * 512], BF16, name="wg", tag="grouped", align_bytes=64)
            wgs[t] = wg
            words = wk[:].rearrange("m k u a e -> m (k u a e)").bitcast(F32).rearrange("m (k u a) -> m k u a", k=NK, u=2)
            transposed(words, wg)

        def w_quant(t, k0, k1):
            quantize_piece(wgs[t], wc, ws, t, k0, k1)

        def c_run(q):
            w1g = stage.tile([P, NK * 512], BF16, name="w1g", tag="grouped", align_bytes=64)
            w1gs[q] = w1g
            words = w1raw[q][:].bitcast(F32).rearrange("m (k a u) -> m k u a", k=NK, u=2)
            transposed(words, w1g)

        def c_quant(q, k0, k1):
            quantize_piece(w1gs[q], w1c, w1s, q, k0, k1)

        zs = {}

        def stage1_passes(k):
            z = work.tile([P, 4, HW], BF16, name="z", tag="bank")
            zs[k] = z
            for t in range(4):
                c0 = (t * NK + k) * P
                nc.tensor.matmul_mx(
                    out=z[:, t, :],
                    lhsT=wc[:, c0 : c0 + P].bitcast(FP8X4),
                    lhsT_scale=ws[:, c0 : c0 + P],
                    rhs=xc[:].bitcast(FP8X4),
                    rhs_scale=xs[:],
                    start=True,
                    stop=True,
                )

        def stage1_relu(k):
            z = zs[k]
            dst = h0all[:, k, 1:17, :, :].rearrange("p a b t -> p (a b) t")
            if k in (1, 3, 5):
                nc.vector.tensor_scalar_max(out=dst, in0=z[:].rearrange("p t n -> p n t"), scalar1=0.0)
            else:
                nc.scalar.activation(out=dst, in_=z[:].rearrange("p t n -> p n t"), func=RELU)

        def stage1(k):
            stage1_passes(k)
            stage1_relu(k)

        ring_order = [k for k in K_ORDER if k < 8]
        slot_of = {}

        def shift_upto(n):
            while len(slot_of) < min(n, 8):
                k = ring_order[len(slot_of)]
                s = len(slot_of) % NSET
                slot_of[k] = s
                if len(slot_of) == 1:
                    nc.gpsimd.memset(hxall[:, 2 * s, 1:17, 14:16, :], 0.0)
                    nc.gpsimd.memset(hxall[:, 2 * s + 1, 1:17, 0:2, :], 0.0)
                    nc.vector.tensor_copy(out=hxall[:, 2 * s, 1:17, 0:15, :], in_=h0all[:, k, 1:17, 1:16, :])
                    nc.vector.tensor_copy(out=hxall[:, 2 * s + 1, 1:17, 1:16, :], in_=h0all[:, k, 1:17, 0:15, :])
                    continue
                flat = h0all[:, k].rearrange("p a b t -> p (a b t)")
                plus = hxall[:, 2 * s].rearrange("p a b t -> p (a b t)")
                minus = hxall[:, 2 * s + 1].rearrange("p a b t -> p (a b t)")
                nc.sync.dma_start(out=plus[:, ROW : ROW + 4 * HW - 4], in_=flat[:, ROW + 4 : ROW + 4 * HW])
                nc.sync.dma_start(out=minus[:, ROW + 4 : ROW + 4 * HW], in_=flat[:, ROW : ROW + 4 * HW - 4])
                nc.gpsimd.memset(hxall[:, 2 * s, 1:17, 15, :], 0.0)
                nc.gpsimd.memset(hxall[:, 2 * s + 1, 1:17, 0, :], 0.0)

        hc = {}
        hs = {}

        def versions(k):
            hs[k] = hs_t[len(hc) % NHC]
            hc[k] = hc_t[len(hc) % NHC]
            for v in range(4):
                dy, dx = RING[(k + 2 * v) % 8]
                if dx == 0:
                    image = h0all[:, k]
                elif dx == 1:
                    image = hxall[:, 2 * slot_of[k]]
                else:
                    image = hxall[:, 2 * slot_of[k] + 1]
                flat = image.rearrange("p a b t -> p (a b t)")
                nc.vector.quantize_mx(
                    out=hc[k][:, v * HW : (v + 1) * HW].bitcast(FP8X4),
                    scales=hs[k][:, v * HW : (v + 1) * HW],
                    in_=flat[:, (1 + dy) * ROW : (1 + dy) * ROW + 4 * HW],
                )

        def centre_quant():
            nc.vector.quantize_mx(
                out=hc8[:].bitcast(FP8X4),
                scales=hs8[:],
                in_=h0all[:, 8].rearrange("p a b t -> p (a b t)")[:, ROW : ROW + 4 * HW],
            )

        def centre():
            for i in range(2):
                c8 = work.tile([P, 2, HW], F32, name="c8", tag="bank")
                for j in range(2):
                    c0 = ((2 * i + j) * NK + 8) * P
                    nc.tensor.matmul_mx(
                        out=c8[:, j, :],
                        lhsT=w1c[:, c0 : c0 + P].bitcast(FP8X4),
                        lhsT_scale=w1s[:, c0 : c0 + P],
                        rhs=hc8[:].bitcast(FP8X4),
                        rhs_scale=hs8[:],
                        start=True,
                        stop=True,
                    )
                nc.scalar.copy(out=u8sb[:, 2 * i : 2 * i + 2, :], in_=c8[:])

        accs = {}
        passes = {}

        def stage2(q, rp, k):
            if (q, rp) not in accs:
                acc = work.tile([P, 512], F32, name="acc", tag="bank")
                accs[(q, rp)] = acc
                passes[(q, rp)] = 0
            passes[(q, rp)] += 1
            c0 = (q * NK + k) * P
            r0 = rp * 512
            nc.tensor.matmul_mx(
                out=accs[(q, rp)][:],
                lhsT=w1c[:, c0 : c0 + P].bitcast(FP8X4),
                lhsT_scale=w1s[:, c0 : c0 + P],
                rhs=hc[k][:, r0 : r0 + 512].bitcast(FP8X4),
                rhs_scale=hs[k][:, r0 : r0 + 512],
                start=passes[(q, rp)] == 1,
                stop=passes[(q, rp)] == NK - 1,
            )

        osbs = {}

        def finish_group(q, rp):
            if rp not in osbs:
                osb4 = raw.tile([P, 4, 512], F32, name="osb4", tag="raw")
                osbs[rp] = osb4
            osb = osbs[rp][:, q, :]
            nc.vector.tensor_tensor(
                out=osb.rearrange("p (r n) -> p r n", r=2),
                in0=accs[(q, rp)][:].rearrange("p (r n) -> p r n", r=2),
                in1=u8sb[:, q : q + 1, :].to_broadcast([P, 2, HW]),
                op=mybir.AluOpType.add,
            )
            nc.sync.dma_start(out=out_v[:, q, rp * 512 : (rp + 1) * 512], in_=osb)

        groups = [(q, rp) for q in range(4) for rp in range(2)]

        def sweep(k, some):
            for q, rp in some:
                stage2(q, rp, k)

        with tc.manual_schedule(engines={mybir.EngineType.PE}):
            burst(N_WARM, dummy[:, 0:P], dummy[:])
            w_tiles(0)
            w_tiles(1)
            w_tiles(2)
            c_run(0)
            w_tiles(3)
            c_run(1)
            c_run(2)
            x_prep()
            for t in range(3):
                w_quant(t, 0, 4)
            w_quant(3, 0, 2)
            w_quant(3, 2, 4)
            for k in range(0, 4):
                stage1(k)
            shift_upto(NSET)
            for t in range(4):
                w_quant(t, 8, 9)
                w_quant(t, 4, 8)
            stage1(8)
            stage1(4)
            stage1(5)
            stage1_passes(6)
            stage1_passes(7)
            c_quant(0, 0, 4)
            c_quant(1, 0, 4)
            versions(K_ORDER[0])
            shift_upto(NSET + 1)
            c_run(3)
            c_quant(2, 0, 4)
            centre_quant()
            for q in range(4):
                c_quant(q, 8, 9)
            for i, k in enumerate(K_ORDER[0:6]):
                if i > 0:
                    if k == 4:
                        for q in range(4):
                            c_quant(q, 4, 8)
                    versions(k)
                    shift_upto(NSET + 1 + i)
                if i == 1:
                    c_quant(3, 0, 4)
                if i == 0:
                    sweep(k, groups[0:6:2])
                    sweep(k, groups[1:6:2])
                elif i < LATE:
                    sweep(k, groups[0:6])
                if i < LATE:
                    if i == 0:
                        stage1_relu(6)
                        stage1_relu(7)
                    if i == LATE - 2:
                        centre()
                    if i == LATE - 1:
                        for kk in K_ORDER[0:LATE]:
                            sweep(kk, groups[6:8])
                else:
                    sweep(k, groups)
            versions(K_ORDER[6])
            versions(K_ORDER[7])
            for rp in range(2):
                for q in range(4):
                    stage2(q, rp, K_ORDER[6])
                    stage2(q, rp, K_ORDER[7])
                    finish_group(q, rp)
